import numpy as np
import ml_dtypes

BF16 = ml_dtypes.bfloat16


def bf(x):
    return np.asarray(x, np.float32).astype(BF16)


def f32(x):
    return np.asarray(x, np.float32)


def f64(x):
    return np.asarray(x).astype(np.float64)


def striped(idx):
    return np.tile(idx.reshape(-1, 16).T, (8, 1))


C, S, B, L, N = 256, 1024, 16, 128, 2048
WSC = 1.5


def setup_inputs():
    return {"x": f32(np.random.standard_normal((C, S))), "wv": f32(WSC * np.random.standard_normal((C, 1)) / np.sqrt(C)), "offs": striped(np.random.permutation(np.tile(np.arange(S), 2))[:N])}


def reference(x, wv, offs):
    idx = offs[:16].T.reshape(-1)
    v = f64(x)[:, idx].reshape(C, B, L)
    t = (f64(wv)[:, :, None] * v).sum(axis=0)
    e = np.exp(t - t.max(axis=1, keepdims=True))
    alpha = e / e.sum(axis=1, keepdims=True)
    return (v * alpha[None, :, :]).sum(axis=2)

@@ -1,0 +1,124 @@
+import concourse.mybir as mybir
+
+F32 = mybir.dt.float32
+BF16 = mybir.dt.bfloat16
+U16 = mybir.dt.uint16
+ALU = mybir.AluOpType
+ACT = mybir.ActivationFunctionType
+AXIS_X = mybir.AxisListType.X
+
+P = 128
+FEATURES = 256
+ITEMS = 1024
+SEQUENCES = 16
+LENGTH = 128
+ENTRIES = SEQUENCES * LENGTH
+BLOCKS = FEATURES // P
+GROUP = 4
+PIECE = GROUP * LENGTH
+PIECES = SEQUENCES // GROUP
+PER_COLUMN = 16
+
+FLOPS = 4 * FEATURES * ENTRIES
+
+
+def tile_if4sr_kernel(tc, x, wv, offs, out):
+    nc = tc.nc
+    with (
+        tc.tile_pool(name="held", bufs=1) as held,
+        tc.tile_pool(name="work", bufs=PIECES) as work,
+        tc.psum_pool(name="psum", bufs=PIECES) as psum,
+    ):
+        offsets = held.tile([P, ENTRIES // PER_COLUMN], U16, name="offsets")
+        nc.sync.dma_start(offsets[:], offs)
+        table = [held.tile([P, ITEMS], F32, name=f"table{k}") for k in range(BLOCKS)]
+        for k in range(BLOCKS):
+            nc.scalar.dma_start(table[k][:], x[k * P : (k + 1) * P, :])
+        wv_column = [held.tile([P, 1], F32, name=f"wv_column{k}") for k in range(BLOCKS)]
+        for k in range(BLOCKS):
+            nc.gpsimd.dma_start(wv_column[k][:], wv[k * P : (k + 1) * P, :])
+
+        selector = held.tile([P, GROUP * P], F32, name="selector")
+        nc.gpsimd.memset(selector[:], 0.0)
+        nc.gpsimd.affine_select(
+            out=selector[:],
+            in_=selector[:],
+            compare_op=ALU.not_equal,
+            fill=1.0,
+            base=0,
+            pattern=[[-1, GROUP], [0, P]],
+            channel_multiplier=1,
+        )
+        one_hot = held.tile([P, GROUP * P], F32, name="one_hot")
+        nc.gpsimd.memset(one_hot[:], 0.0)
+        nc.gpsimd.affine_select(
+            out=one_hot[:],
+            in_=one_hot[:],
+            compare_op=ALU.not_equal,
+            fill=1.0,
+            base=0,
+            pattern=[[1, GROUP], [-1, P]],
+            channel_multiplier=0,
+        )
+        weights = [held.tile([P, GROUP * P], BF16, name=f"weights{k}") for k in range(BLOCKS)]
+        for k in range(BLOCKS):
+            nc.vector.tensor_scalar_mul(weights[k][:], one_hot[:], wv_column[k][:, 0:1])
+
+        result = held.tile([P, BLOCKS, SEQUENCES], F32, name="result")
+
+        for piece in range(PIECES):
+            first_column = piece * PIECE // PER_COLUMN
+            piece_offsets = offsets[:, first_column : first_column + PIECE // PER_COLUMN]
+
+            picked = []
+            rounded = []
+            for k in range(BLOCKS):
+                picked.append(work.tile([P, PIECE], F32, name=f"picked{k}"))
+                nc.scalar.activation(picked[k][:], table[k][:].indirect(piece_offsets), ACT.Copy)
+                rounded.append(work.tile([P, PIECE], BF16, name=f"rounded{k}"))
+                nc.gpsimd.tensor_copy(rounded[k][:], picked[k][:])
+
+            scores = psum.tile([P, LENGTH], F32, name="scores")
+            for k in range(BLOCKS):
+                for g in range(GROUP):
+                    nc.tensor.matmul(
+                        scores[:],
+                        lhsT=weights[k][:, g * P : (g + 1) * P],
+                        rhs=rounded[k][:, g * LENGTH : (g + 1) * LENGTH],
+                        start=(k == 0 and g == 0),
+                        stop=(k == BLOCKS - 1 and g == GROUP - 1),
+                    )
+
+            minus_max = work.tile([P, 1], F32, name="minus_max")
+            nc.vector.reduce_max(minus_max[:], scores[:], axis=AXIS_X, negate=True)
+            exps = work.tile([P, LENGTH], F32, name="exps")
+            exp_sum = work.tile([P, 1], F32, name="exp_sum")
+            nc.scalar.activation(
+                exps[:], scores[:], ACT.Exp, bias=minus_max[:, 0:1], scale=1.0, accum_out=exp_sum[:, 0:1]
+            )
+            inverse_sum = work.tile([P, 1], F32, name="inverse_sum")
+            nc.vector.reciprocal(inverse_sum[:], exp_sum[:])
+            alpha = work.tile([P, LENGTH], F32, name="alpha")
+            nc.vector.tensor_scalar_mul(alpha[:], exps[:], inverse_sum[:, 0:1])
+
+            spread = psum.tile([P, PIECE], F32, name="spread")
+            for g in range(GROUP):
+                nc.tensor.matmul(
+                    spread[:, g * LENGTH : (g + 1) * LENGTH],
+                    lhsT=selector[:, g * P : (g + 1) * P],
+                    rhs=alpha[:],
+                    start=True,
+                    stop=True,
+                )
+
+            for k in range(BLOCKS):
+                weighted = work.tile([P, PIECE], F32, name="weighted")
+                nc.vector.tensor_tensor(weighted[:], picked[k][:], spread[:], ALU.mult)
+                nc.vector.tensor_reduce(
+                    result[:, k, piece * GROUP : (piece + 1) * GROUP],
+                    weighted[:].rearrange("p (g l) -> p g l", l=LENGTH),
+                    axis=AXIS_X,
+                    op=ALU.add,
+                )
+
+        nc.sync.dma_start(out.rearrange("(k p) b -> p k b", p=P), result[:])

@@ -14,10 +14,12 @@ SEQUENCES = 16
 LENGTH = 128
 ENTRIES = SEQUENCES * LENGTH
 BLOCKS = FEATURES // P
-GROUP = 4
-PIECE = GROUP * LENGTH
-PIECES = SEQUENCES // GROUP
 PER_COLUMN = 16
+GROUP = 2
+GROUPS = SEQUENCES // GROUP
+GROUP_ENTRIES = GROUP * LENGTH
+PICKED_BYTES = BLOCKS * GROUP_ENTRIES * 4
+AHEAD = 3
 
 FLOPS = 4 * FEATURES * ENTRIES
 
@@ -26,8 +28,10 @@ def tile_if4sr_kernel(tc, x, wv, offs, out):
     nc = tc.nc
     with (
         tc.tile_pool(name="held", bufs=1) as held,
-        tc.tile_pool(name="work", bufs=PIECES) as work,
-        tc.psum_pool(name="psum", bufs=PIECES) as psum,
+        tc.tile_pool(name="placed", bufs=1) as placed,
+        tc.tile_pool(name="work", bufs=AHEAD + 2) as work,
+        tc.psum_pool(name="score_banks", bufs=4) as score_banks,
+        tc.psum_pool(name="spread_banks", bufs=4) as spread_banks,
     ):
         offsets = held.tile([P, ENTRIES // PER_COLUMN], U16, name="offsets")
         nc.sync.dma_start(offsets[:], offs)
@@ -36,10 +40,13 @@ def tile_if4sr_kernel(tc, x, wv, offs, out):
             nc.scalar.dma_start(table[k][:], x[k * P : (k + 1) * P, :])
         wv_column = [held.tile([P, 1], F32, name=f"wv_column{k}") for k in range(BLOCKS)]
         for k in range(BLOCKS):
-            nc.gpsimd.dma_start(wv_column[k][:], wv[k * P : (k + 1) * P, :])
+            nc.sync.dma_start(wv_column[k][:], wv[k * P : (k + 1) * P, :])
 
+        scratch = held.tile([P, 1], F32, name="scratch")
+        nc.vector.memset(scratch[:], 0.0)
+        nc.scalar.activation(scratch[:], scratch[:], ACT.Exp)
         selector = held.tile([P, GROUP * P], F32, name="selector")
-        nc.gpsimd.memset(selector[:], 0.0)
+        nc.vector.memset(selector[:], 0.0)
         nc.gpsimd.affine_select(
             out=selector[:],
             in_=selector[:],
@@ -50,7 +57,7 @@ def tile_if4sr_kernel(tc, x, wv, offs, out):
             channel_multiplier=1,
         )
         one_hot = held.tile([P, GROUP * P], F32, name="one_hot")
-        nc.gpsimd.memset(one_hot[:], 0.0)
+        nc.vector.memset(one_hot[:], 0.0)
         nc.gpsimd.affine_select(
             out=one_hot[:],
             in_=one_hot[:],
@@ -64,61 +71,71 @@ def tile_if4sr_kernel(tc, x, wv, offs, out):
         for k in range(BLOCKS):
             nc.vector.tensor_scalar_mul(weights[k][:], one_hot[:], wv_column[k][:, 0:1])
 
-        result = held.tile([P, BLOCKS, SEQUENCES], F32, name="result")
+        product_sums = held.tile([P, BLOCKS, SEQUENCES], F32, name="product_sums")
+        inverse_sums = held.tile([P, 1, SEQUENCES], F32, name="inverse_sums")
 
-        for piece in range(PIECES):
-            first_column = piece * PIECE // PER_COLUMN
-            piece_offsets = offsets[:, first_column : first_column + PIECE // PER_COLUMN]
-
-            picked = []
-            rounded = []
+        def look_up_and_score(group):
+            first_column = group * GROUP_ENTRIES // PER_COLUMN
+            group_offsets = offsets[:, first_column : first_column + GROUP_ENTRIES // PER_COLUMN]
+            picked = placed.tile(
+                [P, BLOCKS, GROUP_ENTRIES], F32, name=f"picked{group}", offset=group * PICKED_BYTES
+            )
+            rounded = work.tile([P, BLOCKS, GROUP_ENTRIES], BF16, name="rounded")
             for k in range(BLOCKS):
-                picked.append(work.tile([P, PIECE], F32, name=f"picked{k}"))
-                nc.scalar.activation(picked[k][:], table[k][:].indirect(piece_offsets), ACT.Copy)
-                rounded.append(work.tile([P, PIECE], BF16, name=f"rounded{k}"))
-                nc.gpsimd.tensor_copy(rounded[k][:], picked[k][:])
-
-            scores = psum.tile([P, LENGTH], F32, name="scores")
+                nc.scalar.activation(picked[:, k, :], table[k][:].indirect(group_offsets), ACT.Copy)
+                nc.gpsimd.tensor_copy(rounded[:, k, :], picked[:, k, :])
+            scores = score_banks.tile([P, LENGTH], F32, name="scores")
             for k in range(BLOCKS):
                 for g in range(GROUP):
                     nc.tensor.matmul(
                         scores[:],
                         lhsT=weights[k][:, g * P : (g + 1) * P],
-                        rhs=rounded[k][:, g * LENGTH : (g + 1) * LENGTH],
+                        rhs=rounded[:, k, g * LENGTH : (g + 1) * LENGTH],
                         start=(k == 0 and g == 0),
                         stop=(k == BLOCKS - 1 and g == GROUP - 1),
                     )
-
-            minus_max = work.tile([P, 1], F32, name="minus_max")
-            nc.vector.reduce_max(minus_max[:], scores[:], axis=AXIS_X, negate=True)
-            exps = work.tile([P, LENGTH], F32, name="exps")
-            exp_sum = work.tile([P, 1], F32, name="exp_sum")
-            nc.scalar.activation(
-                exps[:], scores[:], ACT.Exp, bias=minus_max[:, 0:1], scale=1.0, accum_out=exp_sum[:, 0:1]
+            minus_max = placed.tile(
+                [P, 1], F32, name=f"minus_max{group}", offset=(group + AHEAD) * PICKED_BYTES
             )
-            inverse_sum = work.tile([P, 1], F32, name="inverse_sum")
-            nc.vector.reciprocal(inverse_sum[:], exp_sum[:])
-            alpha = work.tile([P, LENGTH], F32, name="alpha")
-            nc.vector.tensor_scalar_mul(alpha[:], exps[:], inverse_sum[:, 0:1])
+            nc.vector.reduce_max(minus_max[:], scores[:], axis=AXIS_X, negate=True)
+            return picked, scores, minus_max
 
-            spread = psum.tile([P, PIECE], F32, name="spread")
+        def weigh_and_sum(group, picked, scores, minus_max):
+            exps = work.tile([P, LENGTH + 1], F32, name="exps")
+            nc.scalar.activation(
+                exps[:, 0:LENGTH],
+                scores[:],
+                ACT.Exp,
+                bias=minus_max[:, 0:1],
+                scale=1.0,
+                accum_out=exps[:, LENGTH : LENGTH + 1],
+            )
+            spread = spread_banks.tile([P, GROUP, LENGTH + 1], F32, name="spread")
             for g in range(GROUP):
                 nc.tensor.matmul(
-                    spread[:, g * LENGTH : (g + 1) * LENGTH],
-                    lhsT=selector[:, g * P : (g + 1) * P],
-                    rhs=alpha[:],
-                    start=True,
-                    stop=True,
+                    spread[:, g, :], lhsT=selector[:, g * P : (g + 1) * P], rhs=exps[:], start=True, stop=True
                 )
+            shape = [P, BLOCKS, GROUP, LENGTH]
+            weighted = work.tile(shape, F32, name="weighted")
+            nc.vector.tensor_tensor(
+                weighted[:],
+                picked[:].rearrange("p k (g l) -> p k g l", l=LENGTH),
+                spread[:, :, 0:LENGTH].unsqueeze(1).to_broadcast(shape),
+                ALU.mult,
+            )
+            b0 = group * GROUP
+            nc.vector.tensor_reduce(product_sums[:, :, b0 : b0 + GROUP], weighted[:], axis=AXIS_X, op=ALU.add)
+            nc.vector.reciprocal(inverse_sums[:, 0, b0 : b0 + GROUP], spread[:, :, LENGTH])
 
-            for k in range(BLOCKS):
-                weighted = work.tile([P, PIECE], F32, name="weighted")
-                nc.vector.tensor_tensor(weighted[:], picked[k][:], spread[:], ALU.mult)
-                nc.vector.tensor_reduce(
-                    result[:, k, piece * GROUP : (piece + 1) * GROUP],
-                    weighted[:].rearrange("p (g l) -> p g l", l=LENGTH),
-                    axis=AXIS_X,
-                    op=ALU.add,
-                )
+        scored = []
+        for step in range(GROUPS + AHEAD):
+            if step >= AHEAD:
+                weigh_and_sum(step - AHEAD, *scored[step - AHEAD])
+            if step < GROUPS:
+                scored.append(look_up_and_score(step))
 
+        result = held.tile([P, BLOCKS, SEQUENCES], F32, name="result")
+        nc.vector.tensor_tensor(
+            result[:], product_sums[:], inverse_sums[:].to_broadcast([P, BLOCKS, SEQUENCES]), ALU.mult
+        )
         nc.sync.dma_start(out.rearrange("(k p) b -> p k b", p=P), result[:])

@@ -15,10 +15,10 @@ LENGTH = 128
 ENTRIES = SEQUENCES * LENGTH
 BLOCKS = FEATURES // P
 PER_COLUMN = 16
-GROUP = 2
-GROUPS = SEQUENCES // GROUP
-GROUP_ENTRIES = GROUP * LENGTH
-PICKED_BYTES = BLOCKS * GROUP_ENTRIES * 4
+LARGEST = 2
+GROUP_SIZES = [2] * 7 + [1] * 2
+assert sum(GROUP_SIZES) == SEQUENCES and max(GROUP_SIZES) <= LARGEST
+PICKED_BYTES = BLOCKS * LARGEST * LENGTH * 4
 AHEAD = 3
 
 FLOPS = 4 * FEATURES * ENTRIES
@@ -45,7 +45,7 @@ def tile_if4sr_kernel(tc, x, wv, offs, out):
         scratch = held.tile([P, 1], F32, name="scratch")
         nc.vector.memset(scratch[:], 0.0)
         nc.scalar.activation(scratch[:], scratch[:], ACT.Exp)
-        selector = held.tile([P, GROUP * P], F32, name="selector")
+        selector = held.tile([P, LARGEST * P], F32, name="selector")
         nc.vector.memset(selector[:], 0.0)
         nc.gpsimd.affine_select(
             out=selector[:],
@@ -53,10 +53,10 @@ def tile_if4sr_kernel(tc, x, wv, offs, out):
             compare_op=ALU.not_equal,
             fill=1.0,
             base=0,
-            pattern=[[-1, GROUP], [0, P]],
+            pattern=[[-1, LARGEST], [0, P]],
             channel_multiplier=1,
         )
-        one_hot = held.tile([P, GROUP * P], F32, name="one_hot")
+        one_hot = held.tile([P, LARGEST * P], F32, name="one_hot")
         nc.vector.memset(one_hot[:], 0.0)
         nc.gpsimd.affine_select(
             out=one_hot[:],
@@ -64,43 +64,41 @@ def tile_if4sr_kernel(tc, x, wv, offs, out):
             compare_op=ALU.not_equal,
             fill=1.0,
             base=0,
-            pattern=[[1, GROUP], [-1, P]],
+            pattern=[[1, LARGEST], [-1, P]],
             channel_multiplier=0,
         )
-        weights = [held.tile([P, GROUP * P], BF16, name=f"weights{k}") for k in range(BLOCKS)]
+        weights = [held.tile([P, LARGEST * P], BF16, name=f"weights{k}") for k in range(BLOCKS)]
         for k in range(BLOCKS):
             nc.vector.tensor_scalar_mul(weights[k][:], one_hot[:], wv_column[k][:, 0:1])
 
-        product_sums = held.tile([P, BLOCKS, SEQUENCES], F32, name="product_sums")
-        inverse_sums = held.tile([P, 1, SEQUENCES], F32, name="inverse_sums")
+        result = held.tile([P, BLOCKS, SEQUENCES], F32, name="result")
 
-        def look_up_and_score(group):
-            first_column = group * GROUP_ENTRIES // PER_COLUMN
-            group_offsets = offsets[:, first_column : first_column + GROUP_ENTRIES // PER_COLUMN]
-            picked = placed.tile(
-                [P, BLOCKS, GROUP_ENTRIES], F32, name=f"picked{group}", offset=group * PICKED_BYTES
+        def look_up_and_score(group, first, size):
+            entries = size * LENGTH
+            first_column = first * LENGTH // PER_COLUMN
+            group_offsets = offsets[:, first_column : first_column + entries // PER_COLUMN]
+            picked = placed.tile([P, BLOCKS, entries], F32, name=f"picked{group}", offset=group * PICKED_BYTES)
+            rounded = placed.tile(
+                [P, BLOCKS, entries], BF16, name=f"rounded{group}", offset=(group + AHEAD) * PICKED_BYTES
             )
-            rounded = work.tile([P, BLOCKS, GROUP_ENTRIES], BF16, name="rounded")
             for k in range(BLOCKS):
                 nc.scalar.activation(picked[:, k, :], table[k][:].indirect(group_offsets), ACT.Copy)
                 nc.gpsimd.tensor_copy(rounded[:, k, :], picked[:, k, :])
             scores = score_banks.tile([P, LENGTH], F32, name="scores")
             for k in range(BLOCKS):
-                for g in range(GROUP):
+                for g in range(size):
                     nc.tensor.matmul(
                         scores[:],
                         lhsT=weights[k][:, g * P : (g + 1) * P],
                         rhs=rounded[:, k, g * LENGTH : (g + 1) * LENGTH],
                         start=(k == 0 and g == 0),
-                        stop=(k == BLOCKS - 1 and g == GROUP - 1),
+                        stop=(k == BLOCKS - 1 and g == size - 1),
                     )
-            minus_max = placed.tile(
-                [P, 1], F32, name=f"minus_max{group}", offset=(group + AHEAD) * PICKED_BYTES
-            )
+            minus_max = work.tile([P, 1], F32, name="minus_max")
             nc.vector.reduce_max(minus_max[:], scores[:], axis=AXIS_X, negate=True)
             return picked, scores, minus_max
 
-        def weigh_and_sum(group, picked, scores, minus_max):
+        def weigh_and_sum(first, size, picked, scores, minus_max):
             exps = work.tile([P, LENGTH + 1], F32, name="exps")
             nc.scalar.activation(
                 exps[:, 0:LENGTH],
@@ -110,32 +108,34 @@ def tile_if4sr_kernel(tc, x, wv, offs, out):
                 scale=1.0,
                 accum_out=exps[:, LENGTH : LENGTH + 1],
             )
-            spread = spread_banks.tile([P, GROUP, LENGTH + 1], F32, name="spread")
-            for g in range(GROUP):
+            spread = spread_banks.tile([P, LARGEST, LENGTH + 1], F32, name="spread")
+            for g in range(size):
                 nc.tensor.matmul(
                     spread[:, g, :], lhsT=selector[:, g * P : (g + 1) * P], rhs=exps[:], start=True, stop=True
                 )
-            shape = [P, BLOCKS, GROUP, LENGTH]
-            weighted = work.tile(shape, F32, name="weighted")
-            nc.vector.tensor_tensor(
-                weighted[:],
-                picked[:].rearrange("p k (g l) -> p k g l", l=LENGTH),
-                spread[:, :, 0:LENGTH].unsqueeze(1).to_broadcast(shape),
-                ALU.mult,
-            )
-            b0 = group * GROUP
-            nc.vector.tensor_reduce(product_sums[:, :, b0 : b0 + GROUP], weighted[:], axis=AXIS_X, op=ALU.add)
-            nc.vector.reciprocal(inverse_sums[:, 0, b0 : b0 + GROUP], spread[:, :, LENGTH])
+            inverse_sums = work.tile([P, LARGEST], F32, name="inverse_sums")
+            nc.vector.reciprocal(inverse_sums[:, 0:size], spread[:, 0:size, LENGTH])
+            for k in range(BLOCKS):
+                for g in range(size):
+                    products = work.tile([P, LENGTH], F32, name="products")
+                    nc.vector.scalar_tensor_tensor(
+                        out=products[:],
+                        in0=picked[:, k, g * LENGTH : (g + 1) * LENGTH],
+                        scalar=inverse_sums[:, g : g + 1],
+                        in1=spread[:, g, 0:LENGTH],
+                        op0=ALU.mult,
+                        op1=ALU.mult,
+                        accum_out=result[:, k, first + g : first + g + 1],
+                    )
 
+        groups = len(GROUP_SIZES)
+        firsts = [sum(GROUP_SIZES[:group]) for group in range(groups)]
         scored = []
-        for step in range(GROUPS + AHEAD):
+        for step in range(groups + AHEAD):
             if step >= AHEAD:
-                weigh_and_sum(step - AHEAD, *scored[step - AHEAD])
-            if step < GROUPS:
-                scored.append(look_up_and_score(step))
+                group = step - AHEAD
+                weigh_and_sum(firsts[group], GROUP_SIZES[group], *scored[group])
+            if step < groups:
+                scored.append(look_up_and_score(step, firsts[step], GROUP_SIZES[step]))
 
-        result = held.tile([P, BLOCKS, SEQUENCES], F32, name="result")
-        nc.vector.tensor_tensor(
-            result[:], product_sums[:], inverse_sums[:].to_broadcast([P, BLOCKS, SEQUENCES]), ALU.mult
-        )
         nc.sync.dma_start(out.rearrange("(k p) b -> p k b", p=P), result[:])

@@ -71,7 +71,8 @@ def tile_if4sr_kernel(tc, x, wv, offs, out):
         for k in range(BLOCKS):
             nc.vector.tensor_scalar_mul(weights[k][:], one_hot[:], wv_column[k][:, 0:1])
 
-        result = held.tile([P, BLOCKS, SEQUENCES], F32, name="result")
+        weighted = held.tile([P, BLOCKS, SEQUENCES], F32, name="weighted")
+        inverse_sums = held.tile([P, SEQUENCES], F32, name="inverse_sums")
 
         def look_up_and_score(group, first, size):
             entries = size * LENGTH
@@ -113,19 +114,18 @@ def tile_if4sr_kernel(tc, x, wv, offs, out):
                 nc.tensor.matmul(
                     spread[:, g, :], lhsT=selector[:, g * P : (g + 1) * P], rhs=exps[:], start=True, stop=True
                 )
-            inverse_sums = work.tile([P, LARGEST], F32, name="inverse_sums")
-            nc.vector.reciprocal(inverse_sums[:, 0:size], spread[:, 0:size, LENGTH])
+            nc.vector.reciprocal(inverse_sums[:, first : first + size], spread[:, 0:size, LENGTH])
             for k in range(BLOCKS):
                 for g in range(size):
                     products = work.tile([P, LENGTH], F32, name="products")
                     nc.vector.scalar_tensor_tensor(
                         out=products[:],
                         in0=picked[:, k, g * LENGTH : (g + 1) * LENGTH],
-                        scalar=inverse_sums[:, g : g + 1],
+                        scalar=1.0,
                         in1=spread[:, g, 0:LENGTH],
                         op0=ALU.mult,
                         op1=ALU.mult,
-                        accum_out=result[:, k, first + g : first + g + 1],
+                        accum_out=weighted[:, k, first + g : first + g + 1],
                     )
 
         groups = len(GROUP_SIZES)
@@ -138,4 +138,11 @@ def tile_if4sr_kernel(tc, x, wv, offs, out):
             if step < groups:
                 scored.append(look_up_and_score(step, firsts[step], GROUP_SIZES[step]))
 
+        result = held.tile([P, BLOCKS, SEQUENCES], F32, name="result")
+        nc.vector.tensor_tensor(
+            out=result[:],
+            in0=weighted[:],
+            in1=inverse_sums[:].unsqueeze(1).to_broadcast([P, BLOCKS, SEQUENCES]),
+            op=ALU.mult,
+        )
         nc.sync.dma_start(out.rearrange("(k p) b -> p k b", p=P), result[:])

@@ -109,20 +109,21 @@ def tile_if4sr_kernel(tc, x, wv, offs, out):
                 scale=1.0,
                 accum_out=exps[:, LENGTH : LENGTH + 1],
             )
-            spread = spread_banks.tile([P, LARGEST, LENGTH + 1], F32, name="spread")
             for g in range(size):
+                spread = spread_banks.tile([P, LENGTH + 1], F32, name="spread")
                 nc.tensor.matmul(
-                    spread[:, g, :], lhsT=selector[:, g * P : (g + 1) * P], rhs=exps[:], start=True, stop=True
+                    spread[:], lhsT=selector[:, g * P : (g + 1) * P], rhs=exps[:], start=True, stop=True
                 )
-            nc.vector.reciprocal(inverse_sums[:, first : first + size], spread[:, 0:size, LENGTH])
-            for k in range(BLOCKS):
-                for g in range(size):
+                nc.vector.reciprocal(
+                    inverse_sums[:, first + g : first + g + 1], spread[:, LENGTH : LENGTH + 1]
+                )
+                for k in range(BLOCKS):
                     products = work.tile([P, LENGTH], F32, name="products")
                     nc.vector.scalar_tensor_tensor(
                         out=products[:],
                         in0=picked[:, k, g * LENGTH : (g + 1) * LENGTH],
                         scalar=1.0,
-                        in1=spread[:, g, 0:LENGTH],
+                        in1=spread[:, 0:LENGTH],
                         op0=ALU.mult,
                         op1=ALU.mult,
                         accum_out=weighted[:, k, first + g : first + g + 1],

@@ -19,7 +19,7 @@ LARGEST = 2
 GROUP_SIZES = [2] * 7 + [1] * 2
 assert sum(GROUP_SIZES) == SEQUENCES and max(GROUP_SIZES) <= LARGEST
 PICKED_BYTES = BLOCKS * LARGEST * LENGTH * 4
-AHEAD = 3
+AHEAD = 2
 
 FLOPS = 4 * FEATURES * ENTRIES
 
@@ -79,19 +79,20 @@ def tile_if4sr_kernel(tc, x, wv, offs, out):
             first_column = first * LENGTH // PER_COLUMN
             group_offsets = offsets[:, first_column : first_column + entries // PER_COLUMN]
             picked = placed.tile([P, BLOCKS, entries], F32, name=f"picked{group}", offset=group * PICKED_BYTES)
-            rounded = placed.tile(
-                [P, BLOCKS, entries], BF16, name=f"rounded{group}", offset=(group + AHEAD) * PICKED_BYTES
-            )
+            rounded = [
+                placed.tile([P, entries], BF16, name=f"rounded{group}", offset=(group + AHEAD) * PICKED_BYTES),
+                work.tile([P, entries], BF16, name="rounded_last"),
+            ]
             for k in range(BLOCKS):
                 nc.scalar.activation(picked[:, k, :], table[k][:].indirect(group_offsets), ACT.Copy)
-                nc.gpsimd.tensor_copy(rounded[:, k, :], picked[:, k, :])
+                nc.gpsimd.tensor_copy(rounded[k][:], picked[:, k, :])
             scores = score_banks.tile([P, LENGTH], F32, name="scores")
             for k in range(BLOCKS):
                 for g in range(size):
                     nc.tensor.matmul(
                         scores[:],
                         lhsT=weights[k][:, g * P : (g + 1) * P],
-                        rhs=rounded[:, k, g * LENGTH : (g + 1) * LENGTH],
+                        rhs=rounded[k][:, g * LENGTH : (g + 1) * LENGTH],
                         start=(k == 0 and g == 0),
                         stop=(k == BLOCKS - 1 and g == size - 1),
                     )

import concourse.mybir as mybir

F32 = mybir.dt.float32
BF16 = mybir.dt.bfloat16
U16 = mybir.dt.uint16
ALU = mybir.AluOpType
ACT = mybir.ActivationFunctionType
AXIS_X = mybir.AxisListType.X

P = 128
FEATURES = 256
ITEMS = 1024
SEQUENCES = 16
LENGTH = 128
ENTRIES = SEQUENCES * LENGTH
BLOCKS = FEATURES // P
PER_COLUMN = 16
LARGEST = 2
GROUP_SIZES = [2] * 7 + [1] * 2
assert sum(GROUP_SIZES) == SEQUENCES and max(GROUP_SIZES) <= LARGEST
PICKED_BYTES = BLOCKS * LARGEST * LENGTH * 4
AHEAD = 2

FLOPS = 4 * FEATURES * ENTRIES


def tile_if4sr_kernel(tc, x, wv, offs, out):
    nc = tc.nc
    with (
        tc.tile_pool(name="held", bufs=1) as held,
        tc.tile_pool(name="placed", bufs=1) as placed,
        tc.tile_pool(name="work", bufs=AHEAD + 2) as work,
        tc.psum_pool(name="score_banks", bufs=4) as score_banks,
        tc.psum_pool(name="spread_banks", bufs=4) as spread_banks,
    ):
        offsets = held.tile([P, ENTRIES // PER_COLUMN], U16, name="offsets")
        nc.sync.dma_start(offsets[:], offs)
        table = [held.tile([P, ITEMS], F32, name=f"table{k}") for k in range(BLOCKS)]
        for k in range(BLOCKS):
            nc.scalar.dma_start(table[k][:], x[k * P : (k + 1) * P, :])
        wv_column = [held.tile([P, 1], F32, name=f"wv_column{k}") for k in range(BLOCKS)]
        for k in range(BLOCKS):
            nc.sync.dma_start(wv_column[k][:], wv[k * P : (k + 1) * P, :])

        scratch = held.tile([P, 1], F32, name="scratch")
        nc.vector.memset(scratch[:], 0.0)
        nc.scalar.activation(scratch[:], scratch[:], ACT.Exp)
        selector = held.tile([P, LARGEST * P], F32, name="selector")
        nc.vector.memset(selector[:], 0.0)
        nc.gpsimd.affine_select(
            out=selector[:],
            in_=selector[:],
            compare_op=ALU.not_equal,
            fill=1.0,
            base=0,
            pattern=[[-1, LARGEST], [0, P]],
            channel_multiplier=1,
        )
        one_hot = held.tile([P, LARGEST * P], F32, name="one_hot")
        nc.vector.memset(one_hot[:], 0.0)
        nc.gpsimd.affine_select(
            out=one_hot[:],
            in_=one_hot[:],
            compare_op=ALU.not_equal,
            fill=1.0,
            base=0,
            pattern=[[1, LARGEST], [-1, P]],
            channel_multiplier=0,
        )
        weights = [held.tile([P, LARGEST * P], BF16, name=f"weights{k}") for k in range(BLOCKS)]
        for k in range(BLOCKS):
            nc.vector.tensor_scalar_mul(weights[k][:], one_hot[:], wv_column[k][:, 0:1])

        weighted = held.tile([P, BLOCKS, SEQUENCES], F32, name="weighted")
        inverse_sums = held.tile([P, SEQUENCES], F32, name="inverse_sums")

        def look_up_and_score(group, first, size):
            entries = size * LENGTH
            first_column = first * LENGTH // PER_COLUMN
            group_offsets = offsets[:, first_column : first_column + entries // PER_COLUMN]
            picked = placed.tile([P, BLOCKS, entries], F32, name=f"picked{group}", offset=group * PICKED_BYTES)
            rounded = [
                placed.tile([P, entries], BF16, name=f"rounded{group}", offset=(group + AHEAD) * PICKED_BYTES),
                work.tile([P, entries], BF16, name="rounded_last"),
            ]
            for k in range(BLOCKS):
                nc.scalar.activation(picked[:, k, :], table[k][:].indirect(group_offsets), ACT.Copy)
                nc.gpsimd.tensor_copy(rounded[k][:], picked[:, k, :])
            scores = score_banks.tile([P, LENGTH], F32, name="scores")
            for k in range(BLOCKS):
                for g in range(size):
                    nc.tensor.matmul(
                        scores[:],
                        lhsT=weights[k][:, g * P : (g + 1) * P],
                        rhs=rounded[k][:, g * LENGTH : (g + 1) * LENGTH],
                        start=(k == 0 and g == 0),
                        stop=(k == BLOCKS - 1 and g == size - 1),
                    )
            minus_max = work.tile([P, 1], F32, name="minus_max")
            nc.vector.reduce_max(minus_max[:], scores[:], axis=AXIS_X, negate=True)
            return picked, scores, minus_max

        def weigh_and_sum(first, size, picked, scores, minus_max):
            exps = work.tile([P, LENGTH + 1], F32, name="exps")
            nc.scalar.activation(
                exps[:, 0:LENGTH],
                scores[:],
                ACT.Exp,
                bias=minus_max[:, 0:1],
                scale=1.0,
                accum_out=exps[:, LENGTH : LENGTH + 1],
            )
            for g in range(size):
                spread = spread_banks.tile([P, LENGTH + 1], F32, name="spread")
                nc.tensor.matmul(
                    spread[:], lhsT=selector[:, g * P : (g + 1) * P], rhs=exps[:], start=True, stop=True
                )
                nc.vector.reciprocal(
                    inverse_sums[:, first + g : first + g + 1], spread[:, LENGTH : LENGTH + 1]
                )
                for k in range(BLOCKS):
                    products = work.tile([P, LENGTH], F32, name="products")
                    nc.vector.scalar_tensor_tensor(
                        out=products[:],
                        in0=picked[:, k, g * LENGTH : (g + 1) * LENGTH],
                        scalar=1.0,
                        in1=spread[:, 0:LENGTH],
                        op0=ALU.mult,
                        op1=ALU.mult,
                        accum_out=weighted[:, k, first + g : first + g + 1],
                    )

        groups = len(GROUP_SIZES)
        firsts = [sum(GROUP_SIZES[:group]) for group in range(groups)]
        scored = []
        for step in range(groups + AHEAD):
            if step >= AHEAD:
                group = step - AHEAD
                weigh_and_sum(firsts[group], GROUP_SIZES[group], *scored[group])
            if step < groups:
                scored.append(look_up_and_score(step, firsts[step], GROUP_SIZES[step]))

        result = held.tile([P, BLOCKS, SEQUENCES], F32, name="result")
        nc.vector.tensor_tensor(
            out=result[:],
            in0=weighted[:],
            in1=inverse_sums[:].unsqueeze(1).to_broadcast([P, BLOCKS, SEQUENCES]),
            op=ALU.mult,
        )
        nc.sync.dma_start(out.rearrange("(k p) b -> p k b", p=P), result[:])
